import numpy as np
import ml_dtypes


def mxq(x, axis, fmt="e4m3"):
    dtype, down = {"e4m3": (ml_dtypes.float8_e4m3fn, 7), "e5m2": (ml_dtypes.float8_e5m2, 14)}[fmt]
    v = np.moveaxis(np.asarray(x, np.float32).astype(ml_dtypes.bfloat16).astype(np.float64), axis, -1)
    blocks = v.reshape(v.shape[:-1] + (-1, 32))
    amax = np.abs(blocks).max(-1, keepdims=True)
    byte = np.maximum(np.where(amax > 0, np.frexp(amax)[1] - 1 + 127, 0) - down, 1)
    scale = np.exp2(byte - 127.0)
    codes = (blocks / scale).astype(np.float32).astype(dtype).astype(np.float64)
    return np.moveaxis((codes * scale).reshape(v.shape), -1, axis)


WIDE = False


def mx_kscale(k):
    if not WIDE:
        return np.ones(k)
    levels = np.array([10, -10, 5, -5, 0])
    a = np.random.permutation(np.resize(levels, k // 512 * 4)).reshape(k // 512, 4)
    idx = np.arange(k)
    return np.exp2(a[idx // 512, idx % 128 // 32])


BF16 = ml_dtypes.bfloat16


def bf(x):
    return np.asarray(x, np.float32).astype(BF16)


def f64(x):
    return np.asarray(x).astype(np.float64)


E2M1 = np.array([0.0, 0.5, 1.0, 1.5, 2.0, 3.0, 4.0, 6.0, -0.0, -0.5, -1.0, -1.5, -2.0, -3.0, -4.0, -6.0])


def pack_weight(w, fmt):
    k, n = w.shape
    w = f64(bf(w)).reshape(k // 32, 32, n)
    amax = np.abs(w).max(1)
    if fmt == "e4m3":
        byte = np.frexp(amax)[1] - 1 + 127 - 7
    else:
        mant, ex = np.frexp(amax / 6.0)
        byte = np.where(mant > 0.5, ex, ex - 1) + 127
    byte = np.clip(np.where(amax > 0, byte, 1), 1, 254)
    scaled = (w * np.exp2(127.0 - byte)[:, None, :]).reshape(k, n).astype(np.float32)
    by_word = np.ascontiguousarray(scaled.reshape(k // 512, 128, 4, n).transpose(0, 1, 3, 2))
    if fmt == "e4m3":
        words = by_word.astype(ml_dtypes.float8_e4m3fn).view(np.uint8)
    else:
        c = by_word.astype(ml_dtypes.float4_e2m1fn).view(np.uint8) & 0xF
        words = c[..., 0::2] | (c[..., 1::2] << 4)
    return np.ascontiguousarray(words), np.ascontiguousarray(byte.astype(np.uint8).reshape(k // 512, 16, n))


def unpack_weight(words, scales, fmt):
    g, p, n, _ = words.shape
    if fmt == "e4m3":
        vals = np.ascontiguousarray(words).view(ml_dtypes.float8_e4m3fn).astype(np.float64)
    else:
        nib = np.empty((g, p, n, 4), np.uint8)
        nib[..., 0::2] = words & 0xF
        nib[..., 1::2] = words >> 4
        vals = E2M1[nib]
    vals = vals * np.repeat(np.exp2(scales.astype(np.float64) - 127.0), 8, axis=1)[..., None]
    return vals.transpose(0, 1, 3, 2).reshape(g * 512, n)

def pack4(w):
    words, scales = pack_weight(w, "e2m1")
    return words.reshape(words.shape[0], 128, -1), scales


def unpack4(words, scales):
    return unpack_weight(words.reshape(words.shape[0], 128, -1, 2), scales, "e2m1")


B, S, H, E, D, TRAIN_LEN = 1, 1024, 1024, 1536, 128, 512


def silu(v):
    return v / (1.0 + np.exp(-v))


def apply_rotary(x, sin, cos):
    x1, x2 = x[..., 0::2], x[..., 1::2]
    return np.concatenate([x1 * cos - x2 * sin, x1 * sin + x2 * cos], axis=-1)


def setup_inputs():
    s = mx_kscale(H)
    pos = np.arange(S)[:, None]
    inv = np.exp(-np.arange(0, D, 2) / D * np.log(10000.0))
    ang = pos * inv[None, :]
    hidden_states = bf(np.random.standard_normal((B, S, H)) * s)
    words, scales = pack4(np.random.standard_normal((H, 2 * E + D)) / np.sqrt(H) / s[:, None])
    return {"hidden_states": hidden_states,
            "sin": bf(np.sin(ang)[None]),
            "cos": bf(np.cos(ang)[None]),
            "W_i_words": words,
            "W_i_scales": scales,
            "q_scale": bf(1.0 + 0.1 * np.random.standard_normal(D)),
            "k_scale": bf(1.0 + 0.1 * np.random.standard_normal(D))}


def reference(hidden_states, sin, cos, W_i_words, W_i_scales, q_scale, k_scale):
    x = silu(mxq(f64(hidden_states), 2, "e4m3") @ unpack4(W_i_words, W_i_scales))
    u, v, qk = np.split(x, [E, 2 * E], axis=-1)
    sn, cs = f64(sin), f64(cos)
    q = apply_rotary(qk * f64(q_scale), sn, cs)
    k = apply_rotary(qk * f64(k_scale), sn, cs)
    return u, v, q, k

@@ -1,0 +1,201 @@
+from contextlib import ExitStack
+
+import concourse.mybir as mybir
+from concourse.masks import make_identity
+
+F32 = mybir.dt.float32
+BF16 = mybir.dt.bfloat16
+I32 = mybir.dt.int32
+U32 = mybir.dt.uint32
+U8 = mybir.dt.uint8
+FP8X4 = mybir.dt.float8_e4m3fn_x4
+FP4X4 = mybir.dt.float4_e2m1fn_x4
+SILU = mybir.ActivationFunctionType.Silu
+MULT = mybir.AluOpType.mult
+ADD = mybir.AluOpType.add
+
+P = 128
+PACK = 4
+K_PASS = P * PACK
+S = 1024
+H = 1024
+E = 1536
+D = 128
+HALF = D // 2
+N_ALL = 2 * E + D
+TILES = S // P
+PASSES = H // K_PASS
+BLOCK = 512
+QK_COL = 2 * E
+
+FLOPS = 2 * S * H * N_ALL
+
+
+def tile_gatedattentionunit_pa_kernel(
+    tc, hidden_states, sin, cos, W_i_words, W_i_scales, q_scale, k_scale, out_0, out_1, out_2, out_3
+):
+    nc = tc.nc
+
+    x_dram = hidden_states.flatten_outer_dims().rearrange("(p m) k -> p m k", m=TILES)
+    cos_dram = cos.flatten_outer_dims().rearrange("(p m) j -> p (m j)", m=TILES)
+    sin_dram = sin.flatten_outer_dims().rearrange("(p m) j -> p (m j)", m=TILES)
+    u_dram = out_0.flatten_outer_dims().rearrange("(p m) e -> p m e", m=TILES)
+    v_dram = out_1.flatten_outer_dims().rearrange("(p m) e -> p m e", m=TILES)
+    q_dram = out_2.flatten_outer_dims().rearrange("(p m) d -> p (m d)", m=TILES)
+    k_dram = out_3.flatten_outer_dims().rearrange("(p m) d -> p (m d)", m=TILES)
+    words_dram = W_i_words.bitcast(I32).rearrange("g p w -> p g w")
+    scales_dram = W_i_scales.bitcast(I32).rearrange("g q w -> q g w")
+
+    with ExitStack() as ctx:
+        keep = ctx.enter_context(tc.tile_pool(name="keep", bufs=1))
+        stage = ctx.enter_context(tc.tile_pool(name="stage", bufs=2))
+        results = ctx.enter_context(tc.tile_pool(name="results", bufs=2 * TILES))
+        flipped = ctx.enter_context(tc.psum_pool(name="flipped", bufs=2))
+        sums = ctx.enter_context(tc.psum_pool(name="sums", bufs=6))
+        ctx.enter_context(tc.manual_schedule())
+
+        x_sb = keep.tile([P, TILES, H], BF16)
+        w_words = keep.tile([P, PASSES, 2 * N_ALL], U8, align_bytes=64)
+        w_scales = keep.tile([P, PASSES, N_ALL], U8, align_bytes=64)
+        x_codes = keep.tile([P, TILES, PASSES * P], U32, align_bytes=64)
+        x_scales = keep.tile([P, TILES, PASSES * P], U8, align_bytes=64)
+        ident = keep.tile([P, P], F32)
+        ones = keep.tile([P, P], BF16)
+        gain_row = keep.tile([P, 2, D], BF16)
+        gains = keep.tile([P, 2, D], F32)
+        table = keep.tile([P, 4, TILES, HALF], BF16)
+        rotated = keep.tile([P, 2, TILES, D], F32)
+        warm = keep.tile([P, 1], F32)
+
+        def load_tokens(first, count):
+            nc.sync.dma_start(out=x_sb[:, first : first + count, :], in_=x_dram[:, first : first + count, :])
+
+        def load_weight_columns(first, width):
+            nc.sync.dma_start(
+                out=w_words[:, :, 2 * first : 2 * (first + width)].bitcast(I32),
+                in_=words_dram[:, :, first // 2 : (first + width) // 2],
+            )
+
+        def load_weight_scales():
+            for b in range(2):
+                for r in range(4):
+                    nc.sync.dma_start(
+                        out=w_scales[32 * b + r : P : 64, :, :].bitcast(I32),
+                        in_=scales_dram[4 * b + r : 16 : 8, :, :],
+                    )
+
+        def transpose_and_quantise(m):
+            x_words = x_sb[:, m, :].bitcast(F32)
+            xt = flipped.tile([P, PASSES, 2, P], F32)
+            for g in range(PASSES):
+                for u in range(2):
+                    nc.tensor.transpose(
+                        xt[:, g, u, :], x_words[:, 256 * g + u : 256 * (g + 1) : 2], ident[:]
+                    )
+            grouped = stage.tile([P, PASSES * P * PACK], BF16, align_bytes=64)
+            nc.vector.tensor_copy(
+                out=grouped[:].bitcast(F32).rearrange("p (g r u) -> p g r u", g=PASSES, u=2),
+                in_=xt[:].rearrange("p g u r -> p g r u"),
+            )
+            nc.vector.quantize_mx(
+                out=x_codes[:, m, :].bitcast(FP8X4), scales=x_scales[:, m, :], in_=grouped[:]
+            )
+
+        def multiply(m, first, width):
+            acc = sums.tile([P, BLOCK], F32, tag="acc")
+            for g in range(PASSES):
+                nc.tensor.matmul_mx(
+                    out=acc[:, 0:width],
+                    lhsT=x_codes[:, m, P * g : P * (g + 1)].bitcast(FP8X4),
+                    lhsT_scale=x_scales[:, m, P * g : P * (g + 1)],
+                    rhs=w_words[:, g, 2 * first : 2 * (first + width)].bitcast(FP4X4),
+                    rhs_scale=w_scales[:, g, first : first + width],
+                    start=(g == 0),
+                    stop=(g == PASSES - 1),
+                )
+            return acc
+
+        def wide_result(m, first, dram):
+            wide = results.tile([P, E], F32, tag="wide")
+            for j in range(E // BLOCK):
+                acc = multiply(m, first + BLOCK * j, BLOCK)
+                nc.scalar.activation(out=wide[:, BLOCK * j : BLOCK * (j + 1)], in_=acc[:], func=SILU)
+            nc.sync.dma_start(out=dram[:, m, :], in_=wide[:])
+
+        def prepare_rotation():
+            spread = sums.tile([P, BLOCK], F32, tag="acc")
+            nc.tensor.matmul(
+                out=spread[:, 0 : 2 * D],
+                lhsT=ones[:],
+                rhs=gain_row[:].rearrange("p a d -> p (a d)"),
+                start=True,
+                stop=True,
+            )
+            nc.vector.tensor_copy(out=gains[:].rearrange("p a d -> p (a d)"), in_=spread[:, 0 : 2 * D])
+            nc.vector.tensor_scalar_mul(out=table[:, 2, :, :], in0=table[:, 1, :, :], scalar1=-1.0)
+            nc.vector.tensor_copy(out=table[:, 3, :, :], in_=table[:, 0, :, :])
+
+        def rotate(m, qk_act):
+            scaled = stage.tile([P, 2, D], F32)
+            nc.vector.tensor_tensor(
+                out=scaled[:], in0=qk_act[:].unsqueeze(1).to_broadcast([P, 2, D]), in1=gains[:], op=MULT
+            )
+            pairs = scaled[:].rearrange("p a (j e) -> p a e j", e=2)
+            from_even = stage.tile([P, 2, 2, HALF], F32)
+            nc.vector.tensor_tensor(
+                out=from_even[:],
+                in0=pairs[:, :, 0, :].unsqueeze(2).to_broadcast([P, 2, 2, HALF]),
+                in1=table[:, 0:2, m, :].unsqueeze(1).to_broadcast([P, 2, 2, HALF]),
+                op=MULT,
+            )
+            from_odd = stage.tile([P, 2, 2, HALF], F32)
+            nc.vector.tensor_tensor(
+                out=from_odd[:],
+                in0=pairs[:, :, 1, :].unsqueeze(2).to_broadcast([P, 2, 2, HALF]),
+                in1=table[:, 2:4, m, :].unsqueeze(1).to_broadcast([P, 2, 2, HALF]),
+                op=MULT,
+            )
+            nc.vector.tensor_tensor(
+                out=rotated[:, :, m, :],
+                in0=from_even[:].rearrange("p a h j -> p a (h j)"),
+                in1=from_odd[:].rearrange("p a h j -> p a (h j)"),
+                op=ADD,
+            )
+
+        nc.vector.memset(w_scales[:].rearrange("p g n -> p (g n)").bitcast(I32), 0)
+        nc.gpsimd.memset(warm[:], 0.0)
+        make_identity(nc, ident[:])
+        nc.gpsimd.memset(gain_row[:], 0.0)
+        nc.gpsimd.memset(ones[:], 1.0)
+        nc.scalar.activation(out=warm[:], in_=warm[:], func=SILU)
+
+        load_tokens(0, 1)
+        load_weight_columns(QK_COL, D)
+        load_weight_columns(0, BLOCK)
+        load_weight_scales()
+        nc.sync.dma_start(out=gain_row[0:1, 0, :], in_=q_scale.unsqueeze(0))
+        nc.sync.dma_start(out=gain_row[0:1, 1, :], in_=k_scale.unsqueeze(0))
+        load_weight_columns(BLOCK, BLOCK)
+        load_weight_columns(2 * BLOCK, BLOCK)
+        load_tokens(1, 1)
+        nc.sync.dma_start(out=table[:, 0, :, :].rearrange("p m j -> p (m j)"), in_=cos_dram)
+        nc.sync.dma_start(out=table[:, 1, :, :].rearrange("p m j -> p (m j)"), in_=sin_dram)
+        load_weight_columns(E, E)
+        load_tokens(2, 2)
+        load_tokens(4, 4)
+
+        transpose_and_quantise(0)
+        for m in range(TILES):
+            acc = multiply(m, QK_COL, D)
+            qk_act = stage.tile([P, D], F32)
+            nc.scalar.activation(out=qk_act[:], in_=acc[:, 0:D], func=SILU)
+            wide_result(m, 0, u_dram)
+            if m + 1 < TILES:
+                transpose_and_quantise(m + 1)
+            if m == 0:
+                prepare_rotation()
+            rotate(m, qk_act)
+            if m == TILES - 1:
+                nc.sync.dma_start(out=q_dram, in_=rotated[:, 0, :, :].rearrange("p m d -> p (m d)"))
+                nc.sync.dma_start(out=k_dram, in_=rotated[:, 1, :, :].rearrange("p m d -> p (m d)"))
+            wide_result(m, E, v_dram)

@@ -27,6 +27,7 @@ TILES = S // P
 PASSES = H // K_PASS
 BLOCK = 512
 QK_COL = 2 * E
+PAIR = 2
 
 FLOPS = 2 * S * H * N_ALL
 
@@ -49,9 +50,9 @@ def tile_gatedattentionunit_pa_kernel(
     with ExitStack() as ctx:
         keep = ctx.enter_context(tc.tile_pool(name="keep", bufs=1))
         stage = ctx.enter_context(tc.tile_pool(name="stage", bufs=2))
+        regroup = ctx.enter_context(tc.tile_pool(name="regroup", bufs=TILES // PAIR))
         results = ctx.enter_context(tc.tile_pool(name="results", bufs=2 * TILES))
-        flipped = ctx.enter_context(tc.psum_pool(name="flipped", bufs=2))
-        sums = ctx.enter_context(tc.psum_pool(name="sums", bufs=6))
+        banks = ctx.enter_context(tc.psum_pool(name="banks", bufs=8))
         ctx.enter_context(tc.manual_schedule())
 
         x_sb = keep.tile([P, TILES, H], BF16)
@@ -65,10 +66,11 @@ def tile_gatedattentionunit_pa_kernel(
         gains = keep.tile([P, 2, D], F32)
         table = keep.tile([P, 4, TILES, HALF], BF16)
         rotated = keep.tile([P, 2, TILES, D], F32)
+        qk_act = keep.tile([P, TILES, D], F32)
         warm = keep.tile([P, 1], F32)
 
-        def load_tokens(first, count):
-            nc.sync.dma_start(out=x_sb[:, first : first + count, :], in_=x_dram[:, first : first + count, :])
+        def load_tokens(first):
+            nc.sync.dma_start(out=x_sb[:, first : first + PAIR, :], in_=x_dram[:, first : first + PAIR, :])
 
         def load_weight_columns(first, width):
             nc.sync.dma_start(
@@ -77,32 +79,33 @@ def tile_gatedattentionunit_pa_kernel(
             )
 
         def load_weight_scales():
-            for b in range(2):
-                for r in range(4):
-                    nc.sync.dma_start(
-                        out=w_scales[32 * b + r : P : 64, :, :].bitcast(I32),
-                        in_=scales_dram[4 * b + r : 16 : 8, :, :],
-                    )
+            for r in range(4):
+                nc.sync.dma_start(
+                    out=w_scales[r : P : 32, :, :].bitcast(I32), in_=scales_dram[r : 16 : 4, :, :]
+                )
 
-        def transpose_and_quantise(m):
-            x_words = x_sb[:, m, :].bitcast(F32)
-            xt = flipped.tile([P, PASSES, 2, P], F32)
-            for g in range(PASSES):
-                for u in range(2):
-                    nc.tensor.transpose(
-                        xt[:, g, u, :], x_words[:, 256 * g + u : 256 * (g + 1) : 2], ident[:]
-                    )
-            grouped = stage.tile([P, PASSES * P * PACK], BF16, align_bytes=64)
-            nc.vector.tensor_copy(
-                out=grouped[:].bitcast(F32).rearrange("p (g r u) -> p g r u", g=PASSES, u=2),
-                in_=xt[:].rearrange("p g u r -> p g r u"),
-            )
+        def transpose_and_quantise(first):
+            grouped = regroup.tile([P, PAIR, PASSES * P * PACK], BF16, align_bytes=64)
+            for i in range(PAIR):
+                x_words = x_sb[:, first + i, :].bitcast(F32)
+                xt = banks.tile([P, PASSES, 2, P], F32, tag="bank")
+                for g in range(PASSES):
+                    for u in range(2):
+                        nc.tensor.transpose(
+                            xt[:, g, u, :], x_words[:, 256 * g + u : 256 * (g + 1) : 2], ident[:]
+                        )
+                nc.vector.tensor_copy(
+                    out=grouped[:, i, :].bitcast(F32).rearrange("p (g r u) -> p g r u", g=PASSES, u=2),
+                    in_=xt[:].rearrange("p g u r -> p g r u"),
+                )
             nc.vector.quantize_mx(
-                out=x_codes[:, m, :].bitcast(FP8X4), scales=x_scales[:, m, :], in_=grouped[:]
+                out=x_codes[:, first : first + PAIR, :].rearrange("p m c -> p (m c)").bitcast(FP8X4),
+                scales=x_scales[:, first : first + PAIR, :].rearrange("p m c -> p (m c)"),
+                in_=grouped[:].rearrange("p m c -> p (m c)"),
             )
 
         def multiply(m, first, width):
-            acc = sums.tile([P, BLOCK], F32, tag="acc")
+            acc = banks.tile([P, BLOCK], F32, tag="bank")
             for g in range(PASSES):
                 nc.tensor.matmul_mx(
                     out=acc[:, 0:width],
@@ -123,7 +126,7 @@ def tile_gatedattentionunit_pa_kernel(
             nc.sync.dma_start(out=dram[:, m, :], in_=wide[:])
 
         def prepare_rotation():
-            spread = sums.tile([P, BLOCK], F32, tag="acc")
+            spread = banks.tile([P, BLOCK], F32, tag="bank")
             nc.tensor.matmul(
                 out=spread[:, 0 : 2 * D],
                 lhsT=ones[:],
@@ -135,10 +138,10 @@ def tile_gatedattentionunit_pa_kernel(
             nc.vector.tensor_scalar_mul(out=table[:, 2, :, :], in0=table[:, 1, :, :], scalar1=-1.0)
             nc.vector.tensor_copy(out=table[:, 3, :, :], in_=table[:, 0, :, :])
 
-        def rotate(m, qk_act):
+        def rotate(m):
             scaled = stage.tile([P, 2, D], F32)
             nc.vector.tensor_tensor(
-                out=scaled[:], in0=qk_act[:].unsqueeze(1).to_broadcast([P, 2, D]), in1=gains[:], op=MULT
+                out=scaled[:], in0=qk_act[:, m, :].unsqueeze(1).to_broadcast([P, 2, D]), in1=gains[:], op=MULT
             )
             pairs = scaled[:].rearrange("p a (j e) -> p a e j", e=2)
             from_even = stage.tile([P, 2, 2, HALF], F32)
@@ -163,38 +166,35 @@ def tile_gatedattentionunit_pa_kernel(
             )
 
         nc.vector.memset(w_scales[:].rearrange("p g n -> p (g n)").bitcast(I32), 0)
+        nc.gpsimd.memset(gain_row[:], 0.0)
         nc.gpsimd.memset(warm[:], 0.0)
         make_identity(nc, ident[:])
-        nc.gpsimd.memset(gain_row[:], 0.0)
         nc.gpsimd.memset(ones[:], 1.0)
+        nc.scalar.dma_start(out=gain_row[0:1, 0, :], in_=q_scale.unsqueeze(0))
+        nc.scalar.dma_start(out=gain_row[0:1, 1, :], in_=k_scale.unsqueeze(0))
         nc.scalar.activation(out=warm[:], in_=warm[:], func=SILU)
 
-        load_tokens(0, 1)
-        load_weight_columns(QK_COL, D)
-        load_weight_columns(0, BLOCK)
+        load_tokens(0)
+        load_tokens(PAIR)
         load_weight_scales()
-        nc.sync.dma_start(out=gain_row[0:1, 0, :], in_=q_scale.unsqueeze(0))
-        nc.sync.dma_start(out=gain_row[0:1, 1, :], in_=k_scale.unsqueeze(0))
-        load_weight_columns(BLOCK, BLOCK)
-        load_weight_columns(2 * BLOCK, BLOCK)
-        load_tokens(1, 1)
+        load_tokens(2 * PAIR)
+        load_tokens(3 * PAIR)
+        load_weight_columns(QK_COL, D)
+        for j in range(E // BLOCK):
+            load_weight_columns(BLOCK * j, BLOCK)
+        load_weight_columns(E, E)
         nc.sync.dma_start(out=table[:, 0, :, :].rearrange("p m j -> p (m j)"), in_=cos_dram)
         nc.sync.dma_start(out=table[:, 1, :, :].rearrange("p m j -> p (m j)"), in_=sin_dram)
-        load_weight_columns(E, E)
-        load_tokens(2, 2)
-        load_tokens(4, 4)
 
-        transpose_and_quantise(0)
+        for first in range(0, TILES, PAIR):
+            transpose_and_quantise(first)
+        prepare_rotation()
+
         for m in range(TILES):
             acc = multiply(m, QK_COL, D)
-            qk_act = stage.tile([P, D], F32)
-            nc.scalar.activation(out=qk_act[:], in_=acc[:, 0:D], func=SILU)
+            nc.scalar.activation(out=qk_act[:, m, :], in_=acc[:, 0:D], func=SILU)
+            rotate(m)
             wide_result(m, 0, u_dram)
-            if m + 1 < TILES:
-                transpose_and_quantise(m + 1)
-            if m == 0:
-                prepare_rotation()
-            rotate(m, qk_act)
             if m == TILES - 1:
                 nc.sync.dma_start(out=q_dram, in_=rotated[:, 0, :, :].rearrange("p m d -> p (m d)"))
                 nc.sync.dma_start(out=k_dram, in_=rotated[:, 1, :, :].rearrange("p m d -> p (m d)"))

@@ -28,6 +28,8 @@ PASSES = H // K_PASS
 BLOCK = 512
 QK_COL = 2 * E
 PAIR = 2
+QK_GROUP = BLOCK // D
+ROTATION_LAG = 2
 
 FLOPS = 2 * S * H * N_ALL
 
@@ -42,8 +44,8 @@ def tile_gatedattentionunit_pa_kernel(
     sin_dram = sin.flatten_outer_dims().rearrange("(p m) j -> p (m j)", m=TILES)
     u_dram = out_0.flatten_outer_dims().rearrange("(p m) e -> p m e", m=TILES)
     v_dram = out_1.flatten_outer_dims().rearrange("(p m) e -> p m e", m=TILES)
-    q_dram = out_2.flatten_outer_dims().rearrange("(p m) d -> p (m d)", m=TILES)
-    k_dram = out_3.flatten_outer_dims().rearrange("(p m) d -> p (m d)", m=TILES)
+    q_dram = out_2.flatten_outer_dims().rearrange("(p m) d -> p m d", m=TILES)
+    k_dram = out_3.flatten_outer_dims().rearrange("(p m) d -> p m d", m=TILES)
     words_dram = W_i_words.bitcast(I32).rearrange("g p w -> p g w")
     scales_dram = W_i_scales.bitcast(I32).rearrange("g q w -> q g w")
 
@@ -104,11 +106,11 @@ def tile_gatedattentionunit_pa_kernel(
                 in_=grouped[:].rearrange("p m c -> p (m c)"),
             )
 
-        def multiply(m, first, width):
-            acc = banks.tile([P, BLOCK], F32, tag="bank")
+        def multiply(acc, m, first):
+            width = acc.shape[1]
             for g in range(PASSES):
                 nc.tensor.matmul_mx(
-                    out=acc[:, 0:width],
+                    out=acc,
                     lhsT=x_codes[:, m, P * g : P * (g + 1)].bitcast(FP8X4),
                     lhsT_scale=x_scales[:, m, P * g : P * (g + 1)],
                     rhs=w_words[:, g, 2 * first : 2 * (first + width)].bitcast(FP4X4),
@@ -116,14 +118,22 @@ def tile_gatedattentionunit_pa_kernel(
                     start=(g == 0),
                     stop=(g == PASSES - 1),
                 )
-            return acc
 
-        def wide_result(m, first, dram):
+        def narrow_results(first):
+            bank = banks.tile([P, QK_GROUP, D], F32, tag="bank")
+            for i in range(QK_GROUP):
+                multiply(bank[:, i, :], first + i, QK_COL)
+            nc.scalar.activation(out=qk_act[:, first : first + QK_GROUP, :], in_=bank[:], func=SILU)
+
+        def wide_result(m, first, dram, blocks_in_store):
             wide = results.tile([P, E], F32, tag="wide")
             for j in range(E // BLOCK):
-                acc = multiply(m, first + BLOCK * j, BLOCK)
-                nc.scalar.activation(out=wide[:, BLOCK * j : BLOCK * (j + 1)], in_=acc[:], func=SILU)
-            nc.sync.dma_start(out=dram[:, m, :], in_=wide[:])
+                bank = banks.tile([P, BLOCK], F32, tag="bank")
+                multiply(bank[:], m, first + BLOCK * j)
+                nc.scalar.activation(out=wide[:, BLOCK * j : BLOCK * (j + 1)], in_=bank[:], func=SILU)
+                if (j + 1) % blocks_in_store == 0:
+                    cols = slice(BLOCK * (j + 1 - blocks_in_store), BLOCK * (j + 1))
+                    nc.sync.dma_start(out=dram[:, m, cols], in_=wide[:, cols])
 
         def prepare_rotation():
             spread = banks.tile([P, BLOCK], F32, tag="bank")
@@ -138,32 +148,37 @@ def tile_gatedattentionunit_pa_kernel(
             nc.vector.tensor_scalar_mul(out=table[:, 2, :, :], in0=table[:, 1, :, :], scalar1=-1.0)
             nc.vector.tensor_copy(out=table[:, 3, :, :], in_=table[:, 0, :, :])
 
-        def rotate(m):
-            scaled = stage.tile([P, 2, D], F32)
+        def rotate(first):
+            tiles = slice(first, first + QK_GROUP)
+            scaled = stage.tile([P, 2, QK_GROUP, D], F32)
             nc.vector.tensor_tensor(
-                out=scaled[:], in0=qk_act[:, m, :].unsqueeze(1).to_broadcast([P, 2, D]), in1=gains[:], op=MULT
-            )
-            pairs = scaled[:].rearrange("p a (j e) -> p a e j", e=2)
-            from_even = stage.tile([P, 2, 2, HALF], F32)
-            nc.vector.tensor_tensor(
-                out=from_even[:],
-                in0=pairs[:, :, 0, :].unsqueeze(2).to_broadcast([P, 2, 2, HALF]),
-                in1=table[:, 0:2, m, :].unsqueeze(1).to_broadcast([P, 2, 2, HALF]),
+                out=scaled[:],
+                in0=qk_act[:, tiles, :].unsqueeze(1).to_broadcast([P, 2, QK_GROUP, D]),
+                in1=gains[:].unsqueeze(2).to_broadcast([P, 2, QK_GROUP, D]),
                 op=MULT,
             )
-            from_odd = stage.tile([P, 2, 2, HALF], F32)
-            nc.vector.tensor_tensor(
-                out=from_odd[:],
-                in0=pairs[:, :, 1, :].unsqueeze(2).to_broadcast([P, 2, 2, HALF]),
-                in1=table[:, 2:4, m, :].unsqueeze(1).to_broadcast([P, 2, 2, HALF]),
-                op=MULT,
-            )
-            nc.vector.tensor_tensor(
-                out=rotated[:, :, m, :],
-                in0=from_even[:].rearrange("p a h j -> p a (h j)"),
-                in1=from_odd[:].rearrange("p a h j -> p a (h j)"),
-                op=ADD,
-            )
+            for a in range(2):
+                pairs = scaled[:, a, :, :].rearrange("p m (j e) -> p m e j", e=2)
+                from_even = stage.tile([P, QK_GROUP, 2, HALF], F32)
+                nc.vector.tensor_tensor(
+                    out=from_even[:],
+                    in0=pairs[:, :, 0, :].unsqueeze(2).to_broadcast([P, QK_GROUP, 2, HALF]),
+                    in1=table[:, 0:2, tiles, :].rearrange("p h m j -> p m h j"),
+                    op=MULT,
+                )
+                from_odd = stage.tile([P, QK_GROUP, 2, HALF], F32)
+                nc.vector.tensor_tensor(
+                    out=from_odd[:],
+                    in0=pairs[:, :, 1, :].unsqueeze(2).to_broadcast([P, QK_GROUP, 2, HALF]),
+                    in1=table[:, 2:4, tiles, :].rearrange("p h m j -> p m h j"),
+                    op=MULT,
+                )
+                nc.vector.tensor_tensor(
+                    out=rotated[:, a, tiles, :],
+                    in0=from_even[:].rearrange("p m h j -> p m (h j)"),
+                    in1=from_odd[:].rearrange("p m h j -> p m (h j)"),
+                    op=ADD,
+                )
 
         nc.vector.memset(w_scales[:].rearrange("p g n -> p (g n)").bitcast(I32), 0)
         nc.gpsimd.memset(gain_row[:], 0.0)
@@ -174,15 +189,12 @@ def tile_gatedattentionunit_pa_kernel(
         nc.scalar.dma_start(out=gain_row[0:1, 1, :], in_=k_scale.unsqueeze(0))
         nc.scalar.activation(out=warm[:], in_=warm[:], func=SILU)
 
-        load_tokens(0)
-        load_tokens(PAIR)
+        for first in range(0, TILES, PAIR):
+            load_tokens(first)
         load_weight_scales()
-        load_tokens(2 * PAIR)
-        load_tokens(3 * PAIR)
         load_weight_columns(QK_COL, D)
-        for j in range(E // BLOCK):
-            load_weight_columns(BLOCK * j, BLOCK)
-        load_weight_columns(E, E)
+        for first in range(0, QK_COL, BLOCK):
+            load_weight_columns(first, BLOCK)
         nc.sync.dma_start(out=table[:, 0, :, :].rearrange("p m j -> p (m j)"), in_=cos_dram)
         nc.sync.dma_start(out=table[:, 1, :, :].rearrange("p m j -> p (m j)"), in_=sin_dram)
 
@@ -190,12 +202,14 @@ def tile_gatedattentionunit_pa_kernel(
             transpose_and_quantise(first)
         prepare_rotation()
 
+        whole = E // BLOCK
         for m in range(TILES):
-            acc = multiply(m, QK_COL, D)
-            nc.scalar.activation(out=qk_act[:, m, :], in_=acc[:, 0:D], func=SILU)
-            rotate(m)
-            wide_result(m, 0, u_dram)
-            if m == TILES - 1:
-                nc.sync.dma_start(out=q_dram, in_=rotated[:, 0, :, :].rearrange("p m d -> p (m d)"))
-                nc.sync.dma_start(out=k_dram, in_=rotated[:, 1, :, :].rearrange("p m d -> p (m d)"))
-            wide_result(m, E, v_dram)
+            if m % QK_GROUP == 0:
+                narrow_results(m)
+                rotate(m)
+            wide_result(m, 0, u_dram, whole)
+            wide_result(m, E, v_dram, 1 if m == TILES - 1 else whole)
+            if m % QK_GROUP == ROTATION_LAG:
+                tiles = slice(m - ROTATION_LAG, m - ROTATION_LAG + QK_GROUP)
+                nc.sync.dma_start(out=q_dram[:, tiles, :], in_=rotated[:, 0, tiles, :])
+                nc.sync.dma_start(out=k_dram[:, tiles, :], in_=rotated[:, 1, tiles, :])

@@ -29,6 +29,7 @@ BLOCK = 512
 QK_COL = 2 * E
 PAIR = 2
 QK_GROUP = BLOCK // D
+COLUMN_BYTES = 2 * PASSES
 ROTATION_LAG = 2
 
 FLOPS = 2 * S * H * N_ALL
@@ -58,7 +59,7 @@ def tile_gatedattentionunit_pa_kernel(
         ctx.enter_context(tc.manual_schedule())
 
         x_sb = keep.tile([P, TILES, H], BF16)
-        w_words = keep.tile([P, PASSES, 2 * N_ALL], U8, align_bytes=64)
+        w_words = keep.tile([P, COLUMN_BYTES * N_ALL], U8, align_bytes=64)
         w_scales = keep.tile([P, PASSES, N_ALL], U8, align_bytes=64)
         x_codes = keep.tile([P, TILES, PASSES * P], U32, align_bytes=64)
         x_scales = keep.tile([P, TILES, PASSES * P], U8, align_bytes=64)
@@ -74,9 +75,13 @@ def tile_gatedattentionunit_pa_kernel(
         def load_tokens(first):
             nc.sync.dma_start(out=x_sb[:, first : first + PAIR, :], in_=x_dram[:, first : first + PAIR, :])
 
-        def load_weight_columns(first, width):
+        def weight_block(first, width):
+            block = w_words[:, COLUMN_BYTES * first : COLUMN_BYTES * (first + width)]
+            return block.rearrange("p (g b) -> p g b", g=PASSES)
+
+        def load_weight_block(first, width):
             nc.sync.dma_start(
-                out=w_words[:, :, 2 * first : 2 * (first + width)].bitcast(I32),
+                out=weight_block(first, width).bitcast(I32),
                 in_=words_dram[:, :, first // 2 : (first + width) // 2],
             )
 
@@ -113,7 +118,7 @@ def tile_gatedattentionunit_pa_kernel(
                     out=acc,
                     lhsT=x_codes[:, m, P * g : P * (g + 1)].bitcast(FP8X4),
                     lhsT_scale=x_scales[:, m, P * g : P * (g + 1)],
-                    rhs=w_words[:, g, 2 * first : 2 * (first + width)].bitcast(FP4X4),
+                    rhs=weight_block(first, width)[:, g, :].bitcast(FP4X4),
                     rhs_scale=w_scales[:, g, first : first + width],
                     start=(g == 0),
                     stop=(g == PASSES - 1),
@@ -192,9 +197,9 @@ def tile_gatedattentionunit_pa_kernel(
         for first in range(0, TILES, PAIR):
             load_tokens(first)
         load_weight_scales()
-        load_weight_columns(QK_COL, D)
+        load_weight_block(QK_COL, D)
         for first in range(0, QK_COL, BLOCK):
-            load_weight_columns(first, BLOCK)
+            load_weight_block(first, BLOCK)
         nc.sync.dma_start(out=table[:, 0, :, :].rearrange("p m j -> p (m j)"), in_=cos_dram)
         nc.sync.dma_start(out=table[:, 1, :, :].rearrange("p m j -> p (m j)"), in_=sin_dram)
 
@@ -207,8 +212,9 @@ def tile_gatedattentionunit_pa_kernel(
             if m % QK_GROUP == 0:
                 narrow_results(m)
                 rotate(m)
-            wide_result(m, 0, u_dram, whole)
-            wide_result(m, E, v_dram, 1 if m == TILES - 1 else whole)
+            blocks_in_store = 1 if m == TILES - 1 else whole
+            wide_result(m, 0, u_dram, blocks_in_store)
+            wide_result(m, E, v_dram, blocks_in_store)
             if m % QK_GROUP == ROTATION_LAG:
                 tiles = slice(m - ROTATION_LAG, m - ROTATION_LAG + QK_GROUP)
                 nc.sync.dma_start(out=q_dram[:, tiles, :], in_=rotated[:, 0, tiles, :])

@@ -27,10 +27,10 @@ TILES = S // P
 PASSES = H // K_PASS
 BLOCK = 512
 QK_COL = 2 * E
-PAIR = 2
 QK_GROUP = BLOCK // D
+EARLY = 3
+WARM_UP = 4
 COLUMN_BYTES = 2 * PASSES
-ROTATION_LAG = 2
 
 FLOPS = 2 * S * H * N_ALL
 
@@ -53,14 +53,15 @@ def tile_gatedattentionunit_pa_kernel(
     with ExitStack() as ctx:
         keep = ctx.enter_context(tc.tile_pool(name="keep", bufs=1))
         stage = ctx.enter_context(tc.tile_pool(name="stage", bufs=2))
-        regroup = ctx.enter_context(tc.tile_pool(name="regroup", bufs=TILES // PAIR))
         results = ctx.enter_context(tc.tile_pool(name="results", bufs=2 * TILES))
         banks = ctx.enter_context(tc.psum_pool(name="banks", bufs=8))
         ctx.enter_context(tc.manual_schedule())
 
         x_sb = keep.tile([P, TILES, H], BF16)
+        grouped = keep.tile([P, TILES, PASSES * P * PACK], BF16, align_bytes=64)
         w_words = keep.tile([P, COLUMN_BYTES * N_ALL], U8, align_bytes=64)
-        w_scales = keep.tile([P, PASSES, N_ALL], U8, align_bytes=64)
+        w_scales_u = keep.tile([P, PASSES, E], U8, align_bytes=64)
+        w_scales_rest = keep.tile([P, PASSES, N_ALL - E], U8, align_bytes=64)
         x_codes = keep.tile([P, TILES, PASSES * P], U32, align_bytes=64)
         x_scales = keep.tile([P, TILES, PASSES * P], U8, align_bytes=64)
         ident = keep.tile([P, P], F32)
@@ -71,9 +72,10 @@ def tile_gatedattentionunit_pa_kernel(
         rotated = keep.tile([P, 2, TILES, D], F32)
         qk_act = keep.tile([P, TILES, D], F32)
         warm = keep.tile([P, 1], F32)
+        spin = keep.tile([P, BLOCK], BF16)
 
-        def load_tokens(first):
-            nc.sync.dma_start(out=x_sb[:, first : first + PAIR, :], in_=x_dram[:, first : first + PAIR, :])
+        def load_tokens(m):
+            nc.sync.dma_start(out=x_sb[:, m, :], in_=x_dram[:, m, :])
 
         def weight_block(first, width):
             block = w_words[:, COLUMN_BYTES * first : COLUMN_BYTES * (first + width)]
@@ -85,16 +87,21 @@ def tile_gatedattentionunit_pa_kernel(
                 in_=words_dram[:, :, first // 2 : (first + width) // 2],
             )
 
-        def load_weight_scales():
+        def load_weight_scales(plane, first, width):
             for r in range(4):
                 nc.sync.dma_start(
-                    out=w_scales[r : P : 32, :, :].bitcast(I32), in_=scales_dram[r : 16 : 4, :, :]
+                    out=plane[r : P : 32, :, :].bitcast(I32),
+                    in_=scales_dram[r : 16 : 4, :, first // 4 : (first + width) // 4],
                 )
 
-        def transpose_and_quantise(first):
-            grouped = regroup.tile([P, PAIR, PASSES * P * PACK], BF16, align_bytes=64)
-            for i in range(PAIR):
-                x_words = x_sb[:, first + i, :].bitcast(F32)
+        def weight_scales(g, first, width):
+            if first < E:
+                return w_scales_u[:, g, first : first + width]
+            return w_scales_rest[:, g, first - E : first - E + width]
+
+        def transpose_and_quantise(first, count):
+            for m in range(first, first + count):
+                x_words = x_sb[:, m, :].bitcast(F32)
                 xt = banks.tile([P, PASSES, 2, P], F32, tag="bank")
                 for g in range(PASSES):
                     for u in range(2):
@@ -102,14 +109,15 @@ def tile_gatedattentionunit_pa_kernel(
                             xt[:, g, u, :], x_words[:, 256 * g + u : 256 * (g + 1) : 2], ident[:]
                         )
                 nc.vector.tensor_copy(
-                    out=grouped[:, i, :].bitcast(F32).rearrange("p (g r u) -> p g r u", g=PASSES, u=2),
+                    out=grouped[:, m, :].bitcast(F32).rearrange("p (g r u) -> p g r u", g=PASSES, u=2),
                     in_=xt[:].rearrange("p g u r -> p g r u"),
                 )
-            nc.vector.quantize_mx(
-                out=x_codes[:, first : first + PAIR, :].rearrange("p m c -> p (m c)").bitcast(FP8X4),
-                scales=x_scales[:, first : first + PAIR, :].rearrange("p m c -> p (m c)"),
-                in_=grouped[:].rearrange("p m c -> p (m c)"),
-            )
+            for m in range(first, first + count):
+                nc.vector.quantize_mx(
+                    out=x_codes[:, m, :].bitcast(FP8X4),
+                    scales=x_scales[:, m, :],
+                    in_=grouped[:, m, :],
+                )
 
         def multiply(acc, m, first):
             width = acc.shape[1]
@@ -119,7 +127,7 @@ def tile_gatedattentionunit_pa_kernel(
                     lhsT=x_codes[:, m, P * g : P * (g + 1)].bitcast(FP8X4),
                     lhsT_scale=x_scales[:, m, P * g : P * (g + 1)],
                     rhs=weight_block(first, width)[:, g, :].bitcast(FP4X4),
-                    rhs_scale=w_scales[:, g, first : first + width],
+                    rhs_scale=weight_scales(g, first, width),
                     start=(g == 0),
                     stop=(g == PASSES - 1),
                 )
@@ -185,7 +193,9 @@ def tile_gatedattentionunit_pa_kernel(
                     op=ADD,
                 )
 
-        nc.vector.memset(w_scales[:].rearrange("p g n -> p (g n)").bitcast(I32), 0)
+        nc.gpsimd.memset(spin[:], 0.0)
+        nc.vector.memset(w_scales_u[:].rearrange("p g n -> p (g n)").bitcast(I32), 0)
+        nc.vector.memset(w_scales_rest[:].rearrange("p g n -> p (g n)").bitcast(I32), 0)
         nc.gpsimd.memset(gain_row[:], 0.0)
         nc.gpsimd.memset(warm[:], 0.0)
         make_identity(nc, ident[:])
@@ -194,28 +204,53 @@ def tile_gatedattentionunit_pa_kernel(
         nc.scalar.dma_start(out=gain_row[0:1, 1, :], in_=k_scale.unsqueeze(0))
         nc.scalar.activation(out=warm[:], in_=warm[:], func=SILU)
 
-        for first in range(0, TILES, PAIR):
-            load_tokens(first)
-        load_weight_scales()
-        load_weight_block(QK_COL, D)
-        for first in range(0, QK_COL, BLOCK):
+        for m in range(EARLY):
+            load_tokens(m)
+        load_weight_scales(w_scales_u, 0, E)
+        for first in range(0, E, BLOCK):
             load_weight_block(first, BLOCK)
+        load_weight_scales(w_scales_rest, E, N_ALL - E)
+        for first in range(E, QK_COL, BLOCK):
+            load_weight_block(first, BLOCK)
+        load_tokens(EARLY)
+        load_weight_block(QK_COL, D)
+        for m in range(EARLY + 1, TILES):
+            load_tokens(m)
         nc.sync.dma_start(out=table[:, 0, :, :].rearrange("p m j -> p (m j)"), in_=cos_dram)
         nc.sync.dma_start(out=table[:, 1, :, :].rearrange("p m j -> p (m j)"), in_=sin_dram)
 
-        for first in range(0, TILES, PAIR):
-            transpose_and_quantise(first)
-        prepare_rotation()
+        def store_rotated(first):
+            tiles = slice(first, first + QK_GROUP)
+            nc.sync.dma_start(out=q_dram[:, tiles, :], in_=rotated[:, 0, tiles, :])
+            nc.sync.dma_start(out=k_dram[:, tiles, :], in_=rotated[:, 1, tiles, :])
+
+        idle = banks.tile([P, BLOCK], F32, tag="bank")
+        for i in range(WARM_UP):
+            nc.tensor.matmul(out=idle[:], lhsT=spin[:, 0:P], rhs=spin[:], start=True, stop=True)
 
         whole = E // BLOCK
-        for m in range(TILES):
-            if m % QK_GROUP == 0:
-                narrow_results(m)
-                rotate(m)
-            blocks_in_store = 1 if m == TILES - 1 else whole
-            wide_result(m, 0, u_dram, blocks_in_store)
-            wide_result(m, E, v_dram, blocks_in_store)
-            if m % QK_GROUP == ROTATION_LAG:
-                tiles = slice(m - ROTATION_LAG, m - ROTATION_LAG + QK_GROUP)
-                nc.sync.dma_start(out=q_dram[:, tiles, :], in_=rotated[:, 0, tiles, :])
-                nc.sync.dma_start(out=k_dram[:, tiles, :], in_=rotated[:, 1, tiles, :])
+        for m in range(EARLY):
+            transpose_and_quantise(m, 1)
+        for m in range(EARLY):
+            wide_result(m, 0, u_dram, whole)
+        wide_result(0, E, v_dram, whole)
+        transpose_and_quantise(EARLY, TILES - EARLY)
+        prepare_rotation()
+        for m in range(1, EARLY):
+            wide_result(m, E, v_dram, whole)
+        narrow_results(0)
+        rotate(0)
+        wide_result(3, 0, u_dram, whole)
+        wide_result(3, E, v_dram, whole)
+        narrow_results(QK_GROUP)
+        store_rotated(0)
+        rotate(QK_GROUP)
+        wide_result(4, 0, u_dram, whole)
+        wide_result(4, E, v_dram, whole)
+        wide_result(5, 0, u_dram, whole)
+        store_rotated(QK_GROUP)
+        wide_result(5, E, v_dram, whole)
+        wide_result(6, 0, u_dram, whole)
+        wide_result(6, E, v_dram, whole)
+        wide_result(7, 0, u_dram, 1)
+        wide_result(7, E, v_dram, 1)

@@ -28,8 +28,9 @@ PASSES = H // K_PASS
 BLOCK = 512
 QK_COL = 2 * E
 QK_GROUP = BLOCK // D
-EARLY = 3
-WARM_UP = 4
+EARLY = 4
+WARM_UP = 3
+W_LOADS = ((0, 512), (512, 512), (1024, 512), (3072, 128), (1536, 1536))
 COLUMN_BYTES = 2 * PASSES
 
 FLOPS = 2 * S * H * N_ALL
@@ -58,10 +59,10 @@ def tile_gatedattentionunit_pa_kernel(
         ctx.enter_context(tc.manual_schedule())
 
         x_sb = keep.tile([P, TILES, H], BF16)
+        shuffled = keep.tile([P, TILES - EARLY, H // 2], F32)
         grouped = keep.tile([P, TILES, PASSES * P * PACK], BF16, align_bytes=64)
         w_words = keep.tile([P, COLUMN_BYTES * N_ALL], U8, align_bytes=64)
-        w_scales_u = keep.tile([P, PASSES, E], U8, align_bytes=64)
-        w_scales_rest = keep.tile([P, PASSES, N_ALL - E], U8, align_bytes=64)
+        w_scales = keep.tile([P, PASSES, N_ALL], U8, align_bytes=64)
         x_codes = keep.tile([P, TILES, PASSES * P], U32, align_bytes=64)
         x_scales = keep.tile([P, TILES, PASSES * P], U8, align_bytes=64)
         ident = keep.tile([P, P], F32)
@@ -74,12 +75,13 @@ def tile_gatedattentionunit_pa_kernel(
         warm = keep.tile([P, 1], F32)
         spin = keep.tile([P, BLOCK], BF16)
 
-        def load_tokens(m):
-            nc.sync.dma_start(out=x_sb[:, m, :], in_=x_dram[:, m, :])
+        def load_tokens(first, count):
+            nc.sync.dma_start(out=x_sb[:, first : first + count, :], in_=x_dram[:, first : first + count, :])
 
         def weight_block(first, width):
-            block = w_words[:, COLUMN_BYTES * first : COLUMN_BYTES * (first + width)]
-            return block.rearrange("p (g b) -> p g b", g=PASSES)
+            start, size = [r for r in W_LOADS if r[0] <= first < r[0] + r[1]][0]
+            region = w_words[:, COLUMN_BYTES * start : COLUMN_BYTES * (start + size)]
+            return region.rearrange("p (g b) -> p g b", g=PASSES)[:, :, 2 * (first - start) : 2 * (first - start + width)]
 
         def load_weight_block(first, width):
             nc.sync.dma_start(
@@ -87,37 +89,44 @@ def tile_gatedattentionunit_pa_kernel(
                 in_=words_dram[:, :, first // 2 : (first + width) // 2],
             )
 
-        def load_weight_scales(plane, first, width):
+        def load_weight_scales():
             for r in range(4):
                 nc.sync.dma_start(
-                    out=plane[r : P : 32, :, :].bitcast(I32),
-                    in_=scales_dram[r : 16 : 4, :, first // 4 : (first + width) // 4],
+                    out=w_scales[r : P : 32, :, :].bitcast(I32), in_=scales_dram[r : 16 : 4, :, :]
                 )
 
-        def weight_scales(g, first, width):
-            if first < E:
-                return w_scales_u[:, g, first : first + width]
-            return w_scales_rest[:, g, first - E : first - E + width]
+        def transpose(m):
+            x_words = x_sb[:, m, :].bitcast(F32)
+            xt = banks.tile([P, PASSES, 2, P], F32, tag="bank")
+            for g in range(PASSES):
+                for u in range(2):
+                    nc.tensor.transpose(xt[:, g, u, :], x_words[:, 256 * g + u : 256 * (g + 1) : 2], ident[:])
+            return xt
 
-        def transpose_and_quantise(first, count):
-            for m in range(first, first + count):
-                x_words = x_sb[:, m, :].bitcast(F32)
-                xt = banks.tile([P, PASSES, 2, P], F32, tag="bank")
-                for g in range(PASSES):
-                    for u in range(2):
-                        nc.tensor.transpose(
-                            xt[:, g, u, :], x_words[:, 256 * g + u : 256 * (g + 1) : 2], ident[:]
-                        )
-                nc.vector.tensor_copy(
-                    out=grouped[:, m, :].bitcast(F32).rearrange("p (g r u) -> p g r u", g=PASSES, u=2),
-                    in_=xt[:].rearrange("p g u r -> p g r u"),
-                )
-            for m in range(first, first + count):
-                nc.vector.quantize_mx(
-                    out=x_codes[:, m, :].bitcast(FP8X4),
-                    scales=x_scales[:, m, :],
-                    in_=grouped[:, m, :],
-                )
+        def shuffle_late_tiles():
+            nc.vector.tensor_copy(
+                out=shuffled[:].rearrange("p m (g u r) -> p (m g) u r", g=PASSES, u=2),
+                in_=x_sb[:, EARLY:TILES, :].rearrange("p m k -> p (m k)").bitcast(F32).rearrange("p (a r u) -> p a u r", r=P, u=2),
+            )
+
+        def transpose_shuffled(m):
+            xt = banks.tile([P, PASSES, 2, P], F32, tag="bank")
+            for g in range(PASSES):
+                for u in range(2):
+                    first = P * (2 * g + u)
+                    nc.tensor.transpose(xt[:, g, u, :], shuffled[:, m - EARLY, first : first + P], ident[:])
+            return xt
+
+        def regroup(m, xt, copy):
+            copy(
+                out=grouped[:, m, :].bitcast(F32).rearrange("p (g r u) -> p g r u", g=PASSES, u=2),
+                in_=xt[:].rearrange("p g u r -> p g r u"),
+            )
+
+        def quantise(m):
+            nc.vector.quantize_mx(
+                out=x_codes[:, m, :].bitcast(FP8X4), scales=x_scales[:, m, :], in_=grouped[:, m, :]
+            )
 
         def multiply(acc, m, first):
             width = acc.shape[1]
@@ -127,7 +136,7 @@ def tile_gatedattentionunit_pa_kernel(
                     lhsT=x_codes[:, m, P * g : P * (g + 1)].bitcast(FP8X4),
                     lhsT_scale=x_scales[:, m, P * g : P * (g + 1)],
                     rhs=weight_block(first, width)[:, g, :].bitcast(FP4X4),
-                    rhs_scale=weight_scales(g, first, width),
+                    rhs_scale=w_scales[:, g, first : first + width],
                     start=(g == 0),
                     stop=(g == PASSES - 1),
                 )
@@ -158,99 +167,120 @@ def tile_gatedattentionunit_pa_kernel(
                 stop=True,
             )
             nc.vector.tensor_copy(out=gains[:].rearrange("p a d -> p (a d)"), in_=spread[:, 0 : 2 * D])
+
+        def complete_table():
             nc.vector.tensor_scalar_mul(out=table[:, 2, :, :], in0=table[:, 1, :, :], scalar1=-1.0)
             nc.vector.tensor_copy(out=table[:, 3, :, :], in_=table[:, 0, :, :])
 
-        def rotate(first):
-            tiles = slice(first, first + QK_GROUP)
+        def scale_pairs(first):
             scaled = stage.tile([P, 2, QK_GROUP, D], F32)
             nc.vector.tensor_tensor(
                 out=scaled[:],
-                in0=qk_act[:, tiles, :].unsqueeze(1).to_broadcast([P, 2, QK_GROUP, D]),
+                in0=qk_act[:, first : first + QK_GROUP, :].unsqueeze(1).to_broadcast([P, 2, QK_GROUP, D]),
                 in1=gains[:].unsqueeze(2).to_broadcast([P, 2, QK_GROUP, D]),
                 op=MULT,
             )
-            for a in range(2):
-                pairs = scaled[:, a, :, :].rearrange("p m (j e) -> p m e j", e=2)
-                from_even = stage.tile([P, QK_GROUP, 2, HALF], F32)
-                nc.vector.tensor_tensor(
-                    out=from_even[:],
-                    in0=pairs[:, :, 0, :].unsqueeze(2).to_broadcast([P, QK_GROUP, 2, HALF]),
-                    in1=table[:, 0:2, tiles, :].rearrange("p h m j -> p m h j"),
-                    op=MULT,
-                )
-                from_odd = stage.tile([P, QK_GROUP, 2, HALF], F32)
-                nc.vector.tensor_tensor(
-                    out=from_odd[:],
-                    in0=pairs[:, :, 1, :].unsqueeze(2).to_broadcast([P, QK_GROUP, 2, HALF]),
-                    in1=table[:, 2:4, tiles, :].rearrange("p h m j -> p m h j"),
-                    op=MULT,
-                )
-                nc.vector.tensor_tensor(
-                    out=rotated[:, a, tiles, :],
-                    in0=from_even[:].rearrange("p m h j -> p m (h j)"),
-                    in1=from_odd[:].rearrange("p m h j -> p m (h j)"),
-                    op=ADD,
-                )
+            return scaled
+
+        def rotate(first, a, scaled):
+            tiles = slice(first, first + QK_GROUP)
+            pairs = scaled[:, a, :, :].rearrange("p m (j e) -> p m e j", e=2)
+            from_even = stage.tile([P, QK_GROUP, 2, HALF], F32)
+            nc.vector.tensor_tensor(
+                out=from_even[:],
+                in0=pairs[:, :, 0, :].unsqueeze(2).to_broadcast([P, QK_GROUP, 2, HALF]),
+                in1=table[:, 0:2, tiles, :].rearrange("p h m j -> p m h j"),
+                op=MULT,
+            )
+            from_odd = stage.tile([P, QK_GROUP, 2, HALF], F32)
+            nc.vector.tensor_tensor(
+                out=from_odd[:],
+                in0=pairs[:, :, 1, :].unsqueeze(2).to_broadcast([P, QK_GROUP, 2, HALF]),
+                in1=table[:, 2:4, tiles, :].rearrange("p h m j -> p m h j"),
+                op=MULT,
+            )
+            nc.vector.tensor_tensor(
+                out=rotated[:, a, tiles, :],
+                in0=from_even[:].rearrange("p m h j -> p m (h j)"),
+                in1=from_odd[:].rearrange("p m h j -> p m (h j)"),
+                op=ADD,
+            )
+
+        def store_rotated(first, a):
+            tiles = slice(first, first + QK_GROUP)
+            nc.sync.dma_start(out=(q_dram, k_dram)[a][:, tiles, :], in_=rotated[:, a, tiles, :])
 
         nc.gpsimd.memset(spin[:], 0.0)
-        nc.vector.memset(w_scales_u[:].rearrange("p g n -> p (g n)").bitcast(I32), 0)
-        nc.vector.memset(w_scales_rest[:].rearrange("p g n -> p (g n)").bitcast(I32), 0)
+        nc.vector.memset(w_scales[:].rearrange("p g n -> p (g n)").bitcast(I32), 0)
         nc.gpsimd.memset(gain_row[:], 0.0)
         nc.gpsimd.memset(warm[:], 0.0)
         make_identity(nc, ident[:])
         nc.gpsimd.memset(ones[:], 1.0)
-        nc.scalar.dma_start(out=gain_row[0:1, 0, :], in_=q_scale.unsqueeze(0))
-        nc.scalar.dma_start(out=gain_row[0:1, 1, :], in_=k_scale.unsqueeze(0))
         nc.scalar.activation(out=warm[:], in_=warm[:], func=SILU)
 
-        for m in range(EARLY):
-            load_tokens(m)
-        load_weight_scales(w_scales_u, 0, E)
-        for first in range(0, E, BLOCK):
-            load_weight_block(first, BLOCK)
-        load_weight_scales(w_scales_rest, E, N_ALL - E)
-        for first in range(E, QK_COL, BLOCK):
-            load_weight_block(first, BLOCK)
-        load_tokens(EARLY)
-        load_weight_block(QK_COL, D)
-        for m in range(EARLY + 1, TILES):
-            load_tokens(m)
+        load_tokens(0, 1)
+        load_tokens(1, 1)
+        load_tokens(2, 2)
+        load_weight_scales()
+        for i in range(3):
+            load_weight_block(*W_LOADS[i])
+        load_weight_block(*W_LOADS[3])
+        nc.sync.dma_start(out=gain_row[0:1, 0, :], in_=q_scale.unsqueeze(0))
+        nc.sync.dma_start(out=gain_row[0:1, 1, :], in_=k_scale.unsqueeze(0))
         nc.sync.dma_start(out=table[:, 0, :, :].rearrange("p m j -> p (m j)"), in_=cos_dram)
         nc.sync.dma_start(out=table[:, 1, :, :].rearrange("p m j -> p (m j)"), in_=sin_dram)
-
-        def store_rotated(first):
-            tiles = slice(first, first + QK_GROUP)
-            nc.sync.dma_start(out=q_dram[:, tiles, :], in_=rotated[:, 0, tiles, :])
-            nc.sync.dma_start(out=k_dram[:, tiles, :], in_=rotated[:, 1, tiles, :])
+        load_weight_block(*W_LOADS[4])
+        load_tokens(EARLY, TILES - EARLY)
 
         idle = banks.tile([P, BLOCK], F32, tag="bank")
         for i in range(WARM_UP):
             nc.tensor.matmul(out=idle[:], lhsT=spin[:, 0:P], rhs=spin[:], start=True, stop=True)
 
         whole = E // BLOCK
-        for m in range(EARLY):
-            transpose_and_quantise(m, 1)
-        for m in range(EARLY):
-            wide_result(m, 0, u_dram, whole)
-        wide_result(0, E, v_dram, whole)
-        transpose_and_quantise(EARLY, TILES - EARLY)
-        prepare_rotation()
-        for m in range(1, EARLY):
-            wide_result(m, E, v_dram, whole)
+        by_vector = nc.vector.tensor_copy
+        by_scalar = nc.scalar.copy
+        xt = transpose(0)
+        regroup(0, xt, by_vector)
+        quantise(0)
+        xt = transpose(1)
+        regroup(1, xt, by_scalar)
+        quantise(1)
+        xt = transpose(2)
+        regroup(2, xt, by_vector)
+        xt = transpose(3)
+        regroup(3, xt, by_scalar)
+        quantise(2)
+        quantise(3)
+        complete_table()
+        wide_result(0, 0, u_dram, whole)
         narrow_results(0)
-        rotate(0)
+        prepare_rotation()
+        scaled = scale_pairs(0)
+        rotate(0, 0, scaled)
+        rotate(0, 1, scaled)
+        shuffle_late_tiles()
+        wide_result(1, 0, u_dram, whole)
+        store_rotated(0, 0)
+        store_rotated(0, 1)
+        wide_result(2, 0, u_dram, whole)
         wide_result(3, 0, u_dram, whole)
-        wide_result(3, E, v_dram, whole)
+        wide_result(0, E, v_dram, whole)
+        wide_result(1, E, v_dram, whole)
+        for m in range(EARLY, TILES):
+            xt = transpose_shuffled(m)
+            regroup(m, xt, by_scalar if m < EARLY + 2 else by_vector)
+        for m in range(EARLY, TILES):
+            quantise(m)
+        wide_result(2, E, v_dram, whole)
         narrow_results(QK_GROUP)
-        store_rotated(0)
-        rotate(QK_GROUP)
+        scaled = scale_pairs(QK_GROUP)
+        rotate(QK_GROUP, 0, scaled)
+        rotate(QK_GROUP, 1, scaled)
+        wide_result(3, E, v_dram, whole)
         wide_result(4, 0, u_dram, whole)
+        store_rotated(QK_GROUP, 0)
+        store_rotated(QK_GROUP, 1)
         wide_result(4, E, v_dram, whole)
-        wide_result(5, 0, u_dram, whole)
-        store_rotated(QK_GROUP)
-        wide_result(5, E, v_dram, whole)
-        wide_result(6, 0, u_dram, whole)
-        wide_result(6, E, v_dram, whole)
-        wide_result(7, 0, u_dram, 1)
-        wide_result(7, E, v_dram, 1)
+        for m in range(5, TILES):
+            wide_result(m, 0, u_dram, whole)
+            wide_result(m, E, v_dram, whole)

@@ -281,6 +281,8 @@ def tile_gatedattentionunit_pa_kernel(
         store_rotated(QK_GROUP, 0)
         store_rotated(QK_GROUP, 1)
         wide_result(4, E, v_dram, whole)
-        for m in range(5, TILES):
+        for m in range(5, TILES - 1):
             wide_result(m, 0, u_dram, whole)
             wide_result(m, E, v_dram, whole)
+        wide_result(TILES - 1, 0, u_dram, 1)
+        wide_result(TILES - 1, E, v_dram, 1)

@@ -30,7 +30,7 @@ QK_COL = 2 * E
 QK_GROUP = BLOCK // D
 EARLY = 4
 WARM_UP = 3
-W_LOADS = ((0, 512), (512, 512), (1024, 512), (3072, 128), (1536, 1536))
+W_LOADS = ((0, 512), (512, 512), (1024, 512), (1536, 1664))
 COLUMN_BYTES = 2 * PASSES
 
 FLOPS = 2 * S * H * N_ALL
@@ -62,7 +62,8 @@ def tile_gatedattentionunit_pa_kernel(
         shuffled = keep.tile([P, TILES - EARLY, H // 2], F32)
         grouped = keep.tile([P, TILES, PASSES * P * PACK], BF16, align_bytes=64)
         w_words = keep.tile([P, COLUMN_BYTES * N_ALL], U8, align_bytes=64)
-        w_scales = keep.tile([P, PASSES, N_ALL], U8, align_bytes=64)
+        w_scales_u = keep.tile([P, PASSES, E], U8, align_bytes=64)
+        w_scales_rest = keep.tile([P, PASSES, N_ALL - E], U8, align_bytes=64)
         x_codes = keep.tile([P, TILES, PASSES * P], U32, align_bytes=64)
         x_scales = keep.tile([P, TILES, PASSES * P], U8, align_bytes=64)
         ident = keep.tile([P, P], F32)
@@ -89,11 +90,17 @@ def tile_gatedattentionunit_pa_kernel(
                 in_=words_dram[:, :, first // 2 : (first + width) // 2],
             )
 
-        def load_weight_scales():
+        def load_weight_scales(plane, first, width):
             for r in range(4):
                 nc.sync.dma_start(
-                    out=w_scales[r : P : 32, :, :].bitcast(I32), in_=scales_dram[r : 16 : 4, :, :]
+                    out=plane[r : P : 32, :, :].bitcast(I32),
+                    in_=scales_dram[r : 16 : 4, :, first // 4 : (first + width) // 4],
                 )
+
+        def weight_scales(g, first, width):
+            if first < E:
+                return w_scales_u[:, g, first : first + width]
+            return w_scales_rest[:, g, first - E : first - E + width]
 
         def transpose(m):
             x_words = x_sb[:, m, :].bitcast(F32)
@@ -136,7 +143,7 @@ def tile_gatedattentionunit_pa_kernel(
                     lhsT=x_codes[:, m, P * g : P * (g + 1)].bitcast(FP8X4),
                     lhsT_scale=x_scales[:, m, P * g : P * (g + 1)],
                     rhs=weight_block(first, width)[:, g, :].bitcast(FP4X4),
-                    rhs_scale=w_scales[:, g, first : first + width],
+                    rhs_scale=weight_scales(g, first, width),
                     start=(g == 0),
                     stop=(g == PASSES - 1),
                 )
@@ -211,7 +218,8 @@ def tile_gatedattentionunit_pa_kernel(
             nc.sync.dma_start(out=(q_dram, k_dram)[a][:, tiles, :], in_=rotated[:, a, tiles, :])
 
         nc.gpsimd.memset(spin[:], 0.0)
-        nc.vector.memset(w_scales[:].rearrange("p g n -> p (g n)").bitcast(I32), 0)
+        nc.vector.memset(w_scales_u[:].rearrange("p g n -> p (g n)").bitcast(I32), 0)
+        nc.vector.memset(w_scales_rest[:].rearrange("p g n -> p (g n)").bitcast(I32), 0)
         nc.gpsimd.memset(gain_row[:], 0.0)
         nc.gpsimd.memset(warm[:], 0.0)
         make_identity(nc, ident[:])
@@ -221,16 +229,16 @@ def tile_gatedattentionunit_pa_kernel(
         load_tokens(0, 1)
         load_tokens(1, 1)
         load_tokens(2, 2)
-        load_weight_scales()
+        load_weight_scales(w_scales_u, 0, E)
         for i in range(3):
             load_weight_block(*W_LOADS[i])
+        load_weight_scales(w_scales_rest, E, N_ALL - E)
         load_weight_block(*W_LOADS[3])
-        nc.sync.dma_start(out=gain_row[0:1, 0, :], in_=q_scale.unsqueeze(0))
-        nc.sync.dma_start(out=gain_row[0:1, 1, :], in_=k_scale.unsqueeze(0))
+        load_tokens(EARLY, TILES - EARLY)
         nc.sync.dma_start(out=table[:, 0, :, :].rearrange("p m j -> p (m j)"), in_=cos_dram)
         nc.sync.dma_start(out=table[:, 1, :, :].rearrange("p m j -> p (m j)"), in_=sin_dram)
-        load_weight_block(*W_LOADS[4])
-        load_tokens(EARLY, TILES - EARLY)
+        nc.sync.dma_start(out=gain_row[0:1, 0, :], in_=q_scale.unsqueeze(0))
+        nc.sync.dma_start(out=gain_row[0:1, 1, :], in_=k_scale.unsqueeze(0))
 
         idle = banks.tile([P, BLOCK], F32, tag="bank")
         for i in range(WARM_UP):
@@ -251,38 +259,37 @@ def tile_gatedattentionunit_pa_kernel(
         regroup(3, xt, by_scalar)
         quantise(2)
         quantise(3)
-        complete_table()
-        wide_result(0, 0, u_dram, whole)
+        for m in range(EARLY):
+            wide_result(m, 0, u_dram, whole)
+        shuffle_late_tiles()
         narrow_results(0)
+        wide_result(0, E, v_dram, whole)
+        complete_table()
         prepare_rotation()
         scaled = scale_pairs(0)
         rotate(0, 0, scaled)
-        rotate(0, 1, scaled)
-        shuffle_late_tiles()
-        wide_result(1, 0, u_dram, whole)
-        store_rotated(0, 0)
-        store_rotated(0, 1)
-        wide_result(2, 0, u_dram, whole)
-        wide_result(3, 0, u_dram, whole)
-        wide_result(0, E, v_dram, whole)
         wide_result(1, E, v_dram, whole)
         for m in range(EARLY, TILES):
             xt = transpose_shuffled(m)
             regroup(m, xt, by_scalar if m < EARLY + 2 else by_vector)
         for m in range(EARLY, TILES):
             quantise(m)
+        rotate(0, 1, scaled)
         wide_result(2, E, v_dram, whole)
+        store_rotated(0, 0)
+        wide_result(3, E, v_dram, whole)
+        wide_result(4, 0, u_dram, whole)
+        store_rotated(0, 1)
         narrow_results(QK_GROUP)
         scaled = scale_pairs(QK_GROUP)
         rotate(QK_GROUP, 0, scaled)
         rotate(QK_GROUP, 1, scaled)
-        wide_result(3, E, v_dram, whole)
-        wide_result(4, 0, u_dram, whole)
-        store_rotated(QK_GROUP, 0)
-        store_rotated(QK_GROUP, 1)
         wide_result(4, E, v_dram, whole)
-        for m in range(5, TILES - 1):
-            wide_result(m, 0, u_dram, whole)
-            wide_result(m, E, v_dram, whole)
+        wide_result(5, 0, u_dram, whole)
+        wide_result(5, E, v_dram, whole)
+        store_rotated(QK_GROUP, 0)
+        wide_result(6, 0, u_dram, whole)
+        store_rotated(QK_GROUP, 1)
+        wide_result(6, E, v_dram, whole)
         wide_result(TILES - 1, 0, u_dram, 1)
         wide_result(TILES - 1, E, v_dram, 1)

@@ -28,6 +28,7 @@ PASSES = H // K_PASS
 BLOCK = 512
 QK_COL = 2 * E
 QK_GROUP = BLOCK // D
+PAIR = 2
 EARLY = 4
 WARM_UP = 3
 W_LOADS = ((0, 512), (512, 512), (1024, 512), (1536, 1664))
@@ -54,7 +55,7 @@ def tile_gatedattentionunit_pa_kernel(
     with ExitStack() as ctx:
         keep = ctx.enter_context(tc.tile_pool(name="keep", bufs=1))
         stage = ctx.enter_context(tc.tile_pool(name="stage", bufs=2))
-        results = ctx.enter_context(tc.tile_pool(name="results", bufs=2 * TILES))
+        results = ctx.enter_context(tc.tile_pool(name="results", bufs=2 * TILES // PAIR))
         banks = ctx.enter_context(tc.psum_pool(name="banks", bufs=8))
         ctx.enter_context(tc.manual_schedule())
 
@@ -154,15 +155,14 @@ def tile_gatedattentionunit_pa_kernel(
                 multiply(bank[:, i, :], first + i, QK_COL)
             nc.scalar.activation(out=qk_act[:, first : first + QK_GROUP, :], in_=bank[:], func=SILU)
 
-        def wide_result(m, first, dram, blocks_in_store):
-            wide = results.tile([P, E], F32, tag="wide")
-            for j in range(E // BLOCK):
-                bank = banks.tile([P, BLOCK], F32, tag="bank")
-                multiply(bank[:], m, first + BLOCK * j)
-                nc.scalar.activation(out=wide[:, BLOCK * j : BLOCK * (j + 1)], in_=bank[:], func=SILU)
-                if (j + 1) % blocks_in_store == 0:
-                    cols = slice(BLOCK * (j + 1 - blocks_in_store), BLOCK * (j + 1))
-                    nc.sync.dma_start(out=dram[:, m, cols], in_=wide[:, cols])
+        def wide_results(m, first, dram):
+            wide = results.tile([P, PAIR, E], F32, tag="wide")
+            for i in range(PAIR):
+                for j in range(E // BLOCK):
+                    bank = banks.tile([P, BLOCK], F32, tag="bank")
+                    multiply(bank[:], m + i, first + BLOCK * j)
+                    nc.scalar.activation(out=wide[:, i, BLOCK * j : BLOCK * (j + 1)], in_=bank[:], func=SILU)
+            nc.sync.dma_start(out=dram[:, m : m + PAIR, :], in_=wide[:])
 
         def prepare_rotation():
             spread = banks.tile([P, BLOCK], F32, tag="bank")
@@ -235,16 +235,15 @@ def tile_gatedattentionunit_pa_kernel(
         load_weight_scales(w_scales_rest, E, N_ALL - E)
         load_weight_block(*W_LOADS[3])
         load_tokens(EARLY, TILES - EARLY)
-        nc.sync.dma_start(out=table[:, 0, :, :].rearrange("p m j -> p (m j)"), in_=cos_dram)
-        nc.sync.dma_start(out=table[:, 1, :, :].rearrange("p m j -> p (m j)"), in_=sin_dram)
         nc.sync.dma_start(out=gain_row[0:1, 0, :], in_=q_scale.unsqueeze(0))
         nc.sync.dma_start(out=gain_row[0:1, 1, :], in_=k_scale.unsqueeze(0))
+        nc.sync.dma_start(out=table[:, 0, :, :].rearrange("p m j -> p (m j)"), in_=cos_dram)
+        nc.sync.dma_start(out=table[:, 1, :, :].rearrange("p m j -> p (m j)"), in_=sin_dram)
 
         idle = banks.tile([P, BLOCK], F32, tag="bank")
         for i in range(WARM_UP):
             nc.tensor.matmul(out=idle[:], lhsT=spin[:, 0:P], rhs=spin[:], start=True, stop=True)
 
-        whole = E // BLOCK
         by_vector = nc.vector.tensor_copy
         by_scalar = nc.scalar.copy
         xt = transpose(0)
@@ -259,37 +258,31 @@ def tile_gatedattentionunit_pa_kernel(
         regroup(3, xt, by_scalar)
         quantise(2)
         quantise(3)
-        for m in range(EARLY):
-            wide_result(m, 0, u_dram, whole)
+        wide_results(0, 0, u_dram)
+        wide_results(2, 0, u_dram)
         shuffle_late_tiles()
         narrow_results(0)
-        wide_result(0, E, v_dram, whole)
         complete_table()
         prepare_rotation()
         scaled = scale_pairs(0)
         rotate(0, 0, scaled)
-        wide_result(1, E, v_dram, whole)
+        wide_results(0, E, v_dram)
+        store_rotated(0, 0)
         for m in range(EARLY, TILES):
             xt = transpose_shuffled(m)
             regroup(m, xt, by_scalar if m < EARLY + 2 else by_vector)
         for m in range(EARLY, TILES):
             quantise(m)
         rotate(0, 1, scaled)
-        wide_result(2, E, v_dram, whole)
-        store_rotated(0, 0)
-        wide_result(3, E, v_dram, whole)
-        wide_result(4, 0, u_dram, whole)
+        wide_results(2, E, v_dram)
         store_rotated(0, 1)
+        wide_results(4, 0, u_dram)
         narrow_results(QK_GROUP)
         scaled = scale_pairs(QK_GROUP)
         rotate(QK_GROUP, 0, scaled)
         rotate(QK_GROUP, 1, scaled)
-        wide_result(4, E, v_dram, whole)
-        wide_result(5, 0, u_dram, whole)
-        wide_result(5, E, v_dram, whole)
+        wide_results(4, E, v_dram)
         store_rotated(QK_GROUP, 0)
-        wide_result(6, 0, u_dram, whole)
         store_rotated(QK_GROUP, 1)
-        wide_result(6, E, v_dram, whole)
-        wide_result(TILES - 1, 0, u_dram, 1)
-        wide_result(TILES - 1, E, v_dram, 1)
+        wide_results(6, 0, u_dram)
+        wide_results(6, E, v_dram)

@@ -30,7 +30,7 @@ QK_COL = 2 * E
 QK_GROUP = BLOCK // D
 PAIR = 2
 EARLY = 4
-WARM_UP = 3
+WARM_UP = 4
 W_LOADS = ((0, 512), (512, 512), (1024, 512), (1536, 1664))
 COLUMN_BYTES = 2 * PASSES
 
@@ -241,23 +241,30 @@ def tile_gatedattentionunit_pa_kernel(
         nc.sync.dma_start(out=table[:, 1, :, :].rearrange("p m j -> p (m j)"), in_=sin_dram)
 
         idle = banks.tile([P, BLOCK], F32, tag="bank")
-        for i in range(WARM_UP):
-            nc.tensor.matmul(out=idle[:], lhsT=spin[:, 0:P], rhs=spin[:], start=True, stop=True)
+
+        def spin_tensor_engine(count):
+            for i in range(count):
+                nc.tensor.matmul(out=idle[:], lhsT=spin[:, 0:P], rhs=spin[:], start=True, stop=True)
+
+        spin_tensor_engine(WARM_UP)
 
         by_vector = nc.vector.tensor_copy
         by_scalar = nc.scalar.copy
         xt = transpose(0)
         regroup(0, xt, by_vector)
         quantise(0)
+        spin_tensor_engine(1)
         xt = transpose(1)
         regroup(1, xt, by_scalar)
         quantise(1)
+        spin_tensor_engine(2)
         xt = transpose(2)
         regroup(2, xt, by_vector)
         xt = transpose(3)
         regroup(3, xt, by_scalar)
         quantise(2)
         quantise(3)
+        spin_tensor_engine(2)
         wide_results(0, 0, u_dram)
         wide_results(2, 0, u_dram)
         shuffle_late_tiles()

@@ -31,7 +31,7 @@ QK_GROUP = BLOCK // D
 PAIR = 2
 EARLY = 4
 WARM_UP = 4
-W_LOADS = ((0, 512), (512, 512), (1024, 512), (1536, 1664))
+W_LOADS = ((0, 512), (512, 1024), (1536, 1664))
 COLUMN_BYTES = 2 * PASSES
 
 FLOPS = 2 * S * H * N_ALL
@@ -155,13 +155,15 @@ def tile_gatedattentionunit_pa_kernel(
                 multiply(bank[:, i, :], first + i, QK_COL)
             nc.scalar.activation(out=qk_act[:, first : first + QK_GROUP, :], in_=bank[:], func=SILU)
 
-        def wide_results(m, first, dram):
+        def wide_results(m, first, dram, first_block_first=False):
             wide = results.tile([P, PAIR, E], F32, tag="wide")
-            for i in range(PAIR):
-                for j in range(E // BLOCK):
-                    bank = banks.tile([P, BLOCK], F32, tag="bank")
-                    multiply(bank[:], m + i, first + BLOCK * j)
-                    nc.scalar.activation(out=wide[:, i, BLOCK * j : BLOCK * (j + 1)], in_=bank[:], func=SILU)
+            order = [(i, j) for i in range(PAIR) for j in range(E // BLOCK)]
+            if first_block_first:
+                order = sorted(order, key=lambda ij: (ij[1] > 0, ij[0], ij[1]))
+            for i, j in order:
+                bank = banks.tile([P, BLOCK], F32, tag="bank")
+                multiply(bank[:], m + i, first + BLOCK * j)
+                nc.scalar.activation(out=wide[:, i, BLOCK * j : BLOCK * (j + 1)], in_=bank[:], func=SILU)
             nc.sync.dma_start(out=dram[:, m : m + PAIR, :], in_=wide[:])
 
         def prepare_rotation():
@@ -226,14 +228,12 @@ def tile_gatedattentionunit_pa_kernel(
         nc.gpsimd.memset(ones[:], 1.0)
         nc.scalar.activation(out=warm[:], in_=warm[:], func=SILU)
 
-        load_tokens(0, 1)
-        load_tokens(1, 1)
+        load_tokens(0, 2)
         load_tokens(2, 2)
         load_weight_scales(w_scales_u, 0, E)
-        for i in range(3):
-            load_weight_block(*W_LOADS[i])
+        for block in W_LOADS:
+            load_weight_block(*block)
         load_weight_scales(w_scales_rest, E, N_ALL - E)
-        load_weight_block(*W_LOADS[3])
         load_tokens(EARLY, TILES - EARLY)
         nc.sync.dma_start(out=gain_row[0:1, 0, :], in_=q_scale.unsqueeze(0))
         nc.sync.dma_start(out=gain_row[0:1, 1, :], in_=k_scale.unsqueeze(0))
@@ -265,7 +265,7 @@ def tile_gatedattentionunit_pa_kernel(
         quantise(2)
         quantise(3)
         spin_tensor_engine(2)
-        wide_results(0, 0, u_dram)
+        wide_results(0, 0, u_dram, first_block_first=True)
         wide_results(2, 0, u_dram)
         shuffle_late_tiles()
         narrow_results(0)

from contextlib import ExitStack

import concourse.mybir as mybir
from concourse.masks import make_identity

F32 = mybir.dt.float32
BF16 = mybir.dt.bfloat16
I32 = mybir.dt.int32
U32 = mybir.dt.uint32
U8 = mybir.dt.uint8
FP8X4 = mybir.dt.float8_e4m3fn_x4
FP4X4 = mybir.dt.float4_e2m1fn_x4
SILU = mybir.ActivationFunctionType.Silu
MULT = mybir.AluOpType.mult
ADD = mybir.AluOpType.add

P = 128
PACK = 4
K_PASS = P * PACK
S = 1024
H = 1024
E = 1536
D = 128
HALF = D // 2
N_ALL = 2 * E + D
TILES = S // P
PASSES = H // K_PASS
BLOCK = 512
QK_COL = 2 * E
QK_GROUP = BLOCK // D
PAIR = 2
EARLY = 4
WARM_UP = 4
W_LOADS = ((0, 512), (512, 1024), (1536, 1664))
COLUMN_BYTES = 2 * PASSES

FLOPS = 2 * S * H * N_ALL


def tile_gatedattentionunit_pa_kernel(
    tc, hidden_states, sin, cos, W_i_words, W_i_scales, q_scale, k_scale, out_0, out_1, out_2, out_3
):
    nc = tc.nc

    x_dram = hidden_states.flatten_outer_dims().rearrange("(p m) k -> p m k", m=TILES)
    cos_dram = cos.flatten_outer_dims().rearrange("(p m) j -> p (m j)", m=TILES)
    sin_dram = sin.flatten_outer_dims().rearrange("(p m) j -> p (m j)", m=TILES)
    u_dram = out_0.flatten_outer_dims().rearrange("(p m) e -> p m e", m=TILES)
    v_dram = out_1.flatten_outer_dims().rearrange("(p m) e -> p m e", m=TILES)
    q_dram = out_2.flatten_outer_dims().rearrange("(p m) d -> p m d", m=TILES)
    k_dram = out_3.flatten_outer_dims().rearrange("(p m) d -> p m d", m=TILES)
    words_dram = W_i_words.bitcast(I32).rearrange("g p w -> p g w")
    scales_dram = W_i_scales.bitcast(I32).rearrange("g q w -> q g w")

    with ExitStack() as ctx:
        keep = ctx.enter_context(tc.tile_pool(name="keep", bufs=1))
        stage = ctx.enter_context(tc.tile_pool(name="stage", bufs=2))
        results = ctx.enter_context(tc.tile_pool(name="results", bufs=2 * TILES // PAIR))
        banks = ctx.enter_context(tc.psum_pool(name="banks", bufs=8))
        ctx.enter_context(tc.manual_schedule())

        x_sb = keep.tile([P, TILES, H], BF16)
        shuffled = keep.tile([P, TILES - EARLY, H // 2], F32)
        grouped = keep.tile([P, TILES, PASSES * P * PACK], BF16, align_bytes=64)
        w_words = keep.tile([P, COLUMN_BYTES * N_ALL], U8, align_bytes=64)
        w_scales_u = keep.tile([P, PASSES, E], U8, align_bytes=64)
        w_scales_rest = keep.tile([P, PASSES, N_ALL - E], U8, align_bytes=64)
        x_codes = keep.tile([P, TILES, PASSES * P], U32, align_bytes=64)
        x_scales = keep.tile([P, TILES, PASSES * P], U8, align_bytes=64)
        ident = keep.tile([P, P], F32)
        ones = keep.tile([P, P], BF16)
        gain_row = keep.tile([P, 2, D], BF16)
        gains = keep.tile([P, 2, D], F32)
        table = keep.tile([P, 4, TILES, HALF], BF16)
        rotated = keep.tile([P, 2, TILES, D], F32)
        qk_act = keep.tile([P, TILES, D], F32)
        warm = keep.tile([P, 1], F32)
        spin = keep.tile([P, BLOCK], BF16)

        def load_tokens(first, count):
            nc.sync.dma_start(out=x_sb[:, first : first + count, :], in_=x_dram[:, first : first + count, :])

        def weight_block(first, width):
            start, size = [r for r in W_LOADS if r[0] <= first < r[0] + r[1]][0]
            region = w_words[:, COLUMN_BYTES * start : COLUMN_BYTES * (start + size)]
            return region.rearrange("p (g b) -> p g b", g=PASSES)[:, :, 2 * (first - start) : 2 * (first - start + width)]

        def load_weight_block(first, width):
            nc.sync.dma_start(
                out=weight_block(first, width).bitcast(I32),
                in_=words_dram[:, :, first // 2 : (first + width) // 2],
            )

        def load_weight_scales(plane, first, width):
            for r in range(4):
                nc.sync.dma_start(
                    out=plane[r : P : 32, :, :].bitcast(I32),
                    in_=scales_dram[r : 16 : 4, :, first // 4 : (first + width) // 4],
                )

        def weight_scales(g, first, width):
            if first < E:
                return w_scales_u[:, g, first : first + width]
            return w_scales_rest[:, g, first - E : first - E + width]

        def transpose(m):
            x_words = x_sb[:, m, :].bitcast(F32)
            xt = banks.tile([P, PASSES, 2, P], F32, tag="bank")
            for g in range(PASSES):
                for u in range(2):
                    nc.tensor.transpose(xt[:, g, u, :], x_words[:, 256 * g + u : 256 * (g + 1) : 2], ident[:])
            return xt

        def shuffle_late_tiles():
            nc.vector.tensor_copy(
                out=shuffled[:].rearrange("p m (g u r) -> p (m g) u r", g=PASSES, u=2),
                in_=x_sb[:, EARLY:TILES, :].rearrange("p m k -> p (m k)").bitcast(F32).rearrange("p (a r u) -> p a u r", r=P, u=2),
            )

        def transpose_shuffled(m):
            xt = banks.tile([P, PASSES, 2, P], F32, tag="bank")
            for g in range(PASSES):
                for u in range(2):
                    first = P * (2 * g + u)
                    nc.tensor.transpose(xt[:, g, u, :], shuffled[:, m - EARLY, first : first + P], ident[:])
            return xt

        def regroup(m, xt, copy):
            copy(
                out=grouped[:, m, :].bitcast(F32).rearrange("p (g r u) -> p g r u", g=PASSES, u=2),
                in_=xt[:].rearrange("p g u r -> p g r u"),
            )

        def quantise(m):
            nc.vector.quantize_mx(
                out=x_codes[:, m, :].bitcast(FP8X4), scales=x_scales[:, m, :], in_=grouped[:, m, :]
            )

        def multiply(acc, m, first):
            width = acc.shape[1]
            for g in range(PASSES):
                nc.tensor.matmul_mx(
                    out=acc,
                    lhsT=x_codes[:, m, P * g : P * (g + 1)].bitcast(FP8X4),
                    lhsT_scale=x_scales[:, m, P * g : P * (g + 1)],
                    rhs=weight_block(first, width)[:, g, :].bitcast(FP4X4),
                    rhs_scale=weight_scales(g, first, width),
                    start=(g == 0),
                    stop=(g == PASSES - 1),
                )

        def narrow_results(first):
            bank = banks.tile([P, QK_GROUP, D], F32, tag="bank")
            for i in range(QK_GROUP):
                multiply(bank[:, i, :], first + i, QK_COL)
            nc.scalar.activation(out=qk_act[:, first : first + QK_GROUP, :], in_=bank[:], func=SILU)

        def wide_results(m, first, dram, first_block_first=False):
            wide = results.tile([P, PAIR, E], F32, tag="wide")
            order = [(i, j) for i in range(PAIR) for j in range(E // BLOCK)]
            if first_block_first:
                order = sorted(order, key=lambda ij: (ij[1] > 0, ij[0], ij[1]))
            for i, j in order:
                bank = banks.tile([P, BLOCK], F32, tag="bank")
                multiply(bank[:], m + i, first + BLOCK * j)
                nc.scalar.activation(out=wide[:, i, BLOCK * j : BLOCK * (j + 1)], in_=bank[:], func=SILU)
            nc.sync.dma_start(out=dram[:, m : m + PAIR, :], in_=wide[:])

        def prepare_rotation():
            spread = banks.tile([P, BLOCK], F32, tag="bank")
            nc.tensor.matmul(
                out=spread[:, 0 : 2 * D],
                lhsT=ones[:],
                rhs=gain_row[:].rearrange("p a d -> p (a d)"),
                start=True,
                stop=True,
            )
            nc.vector.tensor_copy(out=gains[:].rearrange("p a d -> p (a d)"), in_=spread[:, 0 : 2 * D])

        def complete_table():
            nc.vector.tensor_scalar_mul(out=table[:, 2, :, :], in0=table[:, 1, :, :], scalar1=-1.0)
            nc.vector.tensor_copy(out=table[:, 3, :, :], in_=table[:, 0, :, :])

        def scale_pairs(first):
            scaled = stage.tile([P, 2, QK_GROUP, D], F32)
            nc.vector.tensor_tensor(
                out=scaled[:],
                in0=qk_act[:, first : first + QK_GROUP, :].unsqueeze(1).to_broadcast([P, 2, QK_GROUP, D]),
                in1=gains[:].unsqueeze(2).to_broadcast([P, 2, QK_GROUP, D]),
                op=MULT,
            )
            return scaled

        def rotate(first, a, scaled):
            tiles = slice(first, first + QK_GROUP)
            pairs = scaled[:, a, :, :].rearrange("p m (j e) -> p m e j", e=2)
            from_even = stage.tile([P, QK_GROUP, 2, HALF], F32)
            nc.vector.tensor_tensor(
                out=from_even[:],
                in0=pairs[:, :, 0, :].unsqueeze(2).to_broadcast([P, QK_GROUP, 2, HALF]),
                in1=table[:, 0:2, tiles, :].rearrange("p h m j -> p m h j"),
                op=MULT,
            )
            from_odd = stage.tile([P, QK_GROUP, 2, HALF], F32)
            nc.vector.tensor_tensor(
                out=from_odd[:],
                in0=pairs[:, :, 1, :].unsqueeze(2).to_broadcast([P, QK_GROUP, 2, HALF]),
                in1=table[:, 2:4, tiles, :].rearrange("p h m j -> p m h j"),
                op=MULT,
            )
            nc.vector.tensor_tensor(
                out=rotated[:, a, tiles, :],
                in0=from_even[:].rearrange("p m h j -> p m (h j)"),
                in1=from_odd[:].rearrange("p m h j -> p m (h j)"),
                op=ADD,
            )

        def store_rotated(first, a):
            tiles = slice(first, first + QK_GROUP)
            nc.sync.dma_start(out=(q_dram, k_dram)[a][:, tiles, :], in_=rotated[:, a, tiles, :])

        nc.gpsimd.memset(spin[:], 0.0)
        nc.vector.memset(w_scales_u[:].rearrange("p g n -> p (g n)").bitcast(I32), 0)
        nc.vector.memset(w_scales_rest[:].rearrange("p g n -> p (g n)").bitcast(I32), 0)
        nc.gpsimd.memset(gain_row[:], 0.0)
        nc.gpsimd.memset(warm[:], 0.0)
        make_identity(nc, ident[:])
        nc.gpsimd.memset(ones[:], 1.0)
        nc.scalar.activation(out=warm[:], in_=warm[:], func=SILU)

        load_tokens(0, 2)
        load_tokens(2, 2)
        load_weight_scales(w_scales_u, 0, E)
        for block in W_LOADS:
            load_weight_block(*block)
        load_weight_scales(w_scales_rest, E, N_ALL - E)
        load_tokens(EARLY, TILES - EARLY)
        nc.sync.dma_start(out=gain_row[0:1, 0, :], in_=q_scale.unsqueeze(0))
        nc.sync.dma_start(out=gain_row[0:1, 1, :], in_=k_scale.unsqueeze(0))
        nc.sync.dma_start(out=table[:, 0, :, :].rearrange("p m j -> p (m j)"), in_=cos_dram)
        nc.sync.dma_start(out=table[:, 1, :, :].rearrange("p m j -> p (m j)"), in_=sin_dram)

        idle = banks.tile([P, BLOCK], F32, tag="bank")

        def spin_tensor_engine(count):
            for i in range(count):
                nc.tensor.matmul(out=idle[:], lhsT=spin[:, 0:P], rhs=spin[:], start=True, stop=True)

        spin_tensor_engine(WARM_UP)

        by_vector = nc.vector.tensor_copy
        by_scalar = nc.scalar.copy
        xt = transpose(0)
        regroup(0, xt, by_vector)
        quantise(0)
        spin_tensor_engine(1)
        xt = transpose(1)
        regroup(1, xt, by_scalar)
        quantise(1)
        spin_tensor_engine(2)
        xt = transpose(2)
        regroup(2, xt, by_vector)
        xt = transpose(3)
        regroup(3, xt, by_scalar)
        quantise(2)
        quantise(3)
        spin_tensor_engine(2)
        wide_results(0, 0, u_dram, first_block_first=True)
        wide_results(2, 0, u_dram)
        shuffle_late_tiles()
        narrow_results(0)
        complete_table()
        prepare_rotation()
        scaled = scale_pairs(0)
        rotate(0, 0, scaled)
        wide_results(0, E, v_dram)
        store_rotated(0, 0)
        for m in range(EARLY, TILES):
            xt = transpose_shuffled(m)
            regroup(m, xt, by_scalar if m < EARLY + 2 else by_vector)
        for m in range(EARLY, TILES):
            quantise(m)
        rotate(0, 1, scaled)
        wide_results(2, E, v_dram)
        store_rotated(0, 1)
        wide_results(4, 0, u_dram)
        narrow_results(QK_GROUP)
        scaled = scale_pairs(QK_GROUP)
        rotate(QK_GROUP, 0, scaled)
        rotate(QK_GROUP, 1, scaled)
        wide_results(4, E, v_dram)
        store_rotated(QK_GROUP, 0)
        store_rotated(QK_GROUP, 1)
        wide_results(6, 0, u_dram)
        wide_results(6, E, v_dram)
